import numpy as np
import ml_dtypes

BF16 = ml_dtypes.bfloat16


def bf(x):
    return np.asarray(x, np.float32).astype(BF16)


def f32(x):
    return np.asarray(x, np.float32)


def f64(x):
    return np.asarray(x).astype(np.float64)


def striped(idx):
    return np.tile(idx.reshape(-1, 16).T, (8, 1))


D, S, N = 128, 256, 256
TERMS, LIMIT = 150, 6.0


def erf(a):
    c = np.clip(a, -LIMIT, LIMIT)
    term = c.copy()
    total = c.copy()
    for i in range(1, TERMS):
        term = term * 2.0 * c * c / (2.0 * i + 1.0)
        total = total + term
    inner = 2.0 / np.sqrt(np.pi) * np.exp(-c * c) * total
    return np.where(np.abs(a) > LIMIT, np.sign(a), inner)


def gelu_erf(v):
    return 0.5 * v * (1.0 + erf(v / np.sqrt(2.0)))


def setup_inputs():
    return {"table": bf(np.random.standard_normal((D, S))), "x": bf(np.random.standard_normal((D, N))), "w_node": bf(np.random.standard_normal((D, D)) / np.sqrt(3.0 * D)), "w_x": bf(np.random.standard_normal((D, D)) / np.sqrt(3.0 * D)), "b": f32(0.1 * np.random.standard_normal((D, 1))), "offs": striped(np.random.permutation(np.tile(np.arange(S), 2))[:N])}


def reference(table, x, w_node, w_x, b, offs):
    idx = offs[:16].T.reshape(-1)
    pos = f64(w_x)[1::2].sum(axis=0)[:, None]
    pre = f64(w_node).T @ f64(table)[:, idx] + f64(w_x).T @ f64(x) + pos + f64(b)
    return gelu_erf(pre)

@@ -1,0 +1,48 @@
+import concourse.mybir as mybir
+
+BF16 = mybir.dt.bfloat16
+F32 = mybir.dt.float32
+I32 = mybir.dt.int32
+U16 = mybir.dt.uint16
+
+D = 128
+S = 256
+N = 256
+
+FLOPS = 2 * D * D * N * 2 + 2 * (D // 2) * D
+
+
+def tile_temporalattention_kernel(tc, table, x, w_node, w_x, b, offs, out):
+    nc = tc.nc
+    with (
+        tc.tile_pool(name="held", bufs=1) as held,
+        tc.psum_pool(name="psum", bufs=1) as psum,
+    ):
+        offsets = held.tile([D, N // 16], U16, name="offsets")
+        nc.sync.dma_start(offsets[:], offs)
+        node_weights = held.tile([D, D], BF16, name="node_weights")
+        nc.sync.dma_start(node_weights[:], w_node)
+        table_tile = held.tile([D, S], BF16, name="table_tile")
+        nc.sync.dma_start(table_tile[:], table)
+        x_weights = held.tile([D, D], BF16, name="x_weights")
+        nc.scalar.dma_start(x_weights[:], w_x)
+        x_tile = held.tile([D, N], BF16, name="x_tile")
+        nc.scalar.dma_start(x_tile[:], x)
+        bias = held.tile([D, 1], F32, name="bias")
+        nc.gpsimd.dma_start(bias[:], b)
+
+        feature = held.tile([D, 1], I32, name="feature")
+        nc.gpsimd.iota(feature[:], pattern=[[0, 1]], base=0, channel_multiplier=1)
+        parity = held.tile([D, 1], I32, name="parity")
+        nc.vector.tensor_single_scalar(parity[:], feature[:], 1, mybir.AluOpType.bitwise_and)
+        position_code = held.tile([D, 1], BF16, name="position_code")
+        nc.vector.tensor_copy(position_code[:], parity[:])
+
+        pre = psum.tile([D, N], F32, name="pre")
+        nc.tensor.matmul(pre[:], x_weights[:], position_code[:].to_broadcast([D, N]), start=True, stop=False)
+        nc.tensor.matmul(pre[:], x_weights[:], x_tile[:], start=False, stop=False)
+        nc.tensor.matmul(pre[:], node_weights[:], table_tile[:].indirect(offsets[:]), start=False, stop=True)
+
+        result = held.tile([D, N], F32, name="result")
+        nc.scalar.activation(result[:], pre[:], mybir.ActivationFunctionType.Gelu, bias=bias[:])
+        nc.sync.dma_start(out, result[:])

@@ -31,6 +31,10 @@ def tile_temporalattention_kernel(tc, table, x, w_node, w_x, b, offs, out):
         bias = held.tile([D, 1], F32, name="bias")
         nc.gpsimd.dma_start(bias[:], b)
 
+        scratch = held.tile([D, 1], F32, name="scratch")
+        nc.vector.memset(scratch[:], 0.0)
+        nc.scalar.activation(scratch[:], scratch[:], mybir.ActivationFunctionType.Gelu)
+
         feature = held.tile([D, 1], I32, name="feature")
         nc.gpsimd.iota(feature[:], pattern=[[0, 1]], base=0, channel_multiplier=1)
         parity = held.tile([D, 1], I32, name="parity")

@@ -29,7 +29,7 @@ def tile_temporalattention_kernel(tc, table, x, w_node, w_x, b, offs, out):
         x_tile = held.tile([D, N], BF16, name="x_tile")
         nc.scalar.dma_start(x_tile[:], x)
         bias = held.tile([D, 1], F32, name="bias")
-        nc.gpsimd.dma_start(bias[:], b)
+        nc.scalar.dma_start(bias[:], b)
 
         scratch = held.tile([D, 1], F32, name="scratch")
         nc.vector.memset(scratch[:], 0.0)

@@ -18,16 +18,16 @@ def tile_temporalattention_kernel(tc, table, x, w_node, w_x, b, offs, out):
         tc.tile_pool(name="held", bufs=1) as held,
         tc.psum_pool(name="psum", bufs=1) as psum,
     ):
+        x_weights = held.tile([D, D], BF16, name="x_weights")
+        nc.sync.dma_start(x_weights[:], w_x)
+        x_tile = held.tile([D, N], BF16, name="x_tile")
+        nc.sync.dma_start(x_tile[:], x)
         offsets = held.tile([D, N // 16], U16, name="offsets")
         nc.sync.dma_start(offsets[:], offs)
         node_weights = held.tile([D, D], BF16, name="node_weights")
-        nc.sync.dma_start(node_weights[:], w_node)
+        nc.scalar.dma_start(node_weights[:], w_node)
         table_tile = held.tile([D, S], BF16, name="table_tile")
-        nc.sync.dma_start(table_tile[:], table)
-        x_weights = held.tile([D, D], BF16, name="x_weights")
-        nc.scalar.dma_start(x_weights[:], w_x)
-        x_tile = held.tile([D, N], BF16, name="x_tile")
-        nc.scalar.dma_start(x_tile[:], x)
+        nc.scalar.dma_start(table_tile[:], table)
         bias = held.tile([D, 1], F32, name="bias")
         nc.scalar.dma_start(bias[:], b)
 

@@ -2,12 +2,12 @@ import concourse.mybir as mybir
 
 BF16 = mybir.dt.bfloat16
 F32 = mybir.dt.float32
-I32 = mybir.dt.int32
 U16 = mybir.dt.uint16
 
 D = 128
 S = 256
 N = 256
+BLOCK = 32
 
 FLOPS = 2 * D * D * N * 2 + 2 * (D // 2) * D
 
@@ -35,15 +35,15 @@ def tile_temporalattention_kernel(tc, table, x, w_node, w_x, b, offs, out):
         nc.vector.memset(scratch[:], 0.0)
         nc.scalar.activation(scratch[:], scratch[:], mybir.ActivationFunctionType.Gelu)
 
-        feature = held.tile([D, 1], I32, name="feature")
-        nc.gpsimd.iota(feature[:], pattern=[[0, 1]], base=0, channel_multiplier=1)
-        parity = held.tile([D, 1], I32, name="parity")
-        nc.vector.tensor_single_scalar(parity[:], feature[:], 1, mybir.AluOpType.bitwise_and)
-        position_code = held.tile([D, 1], BF16, name="position_code")
-        nc.vector.tensor_copy(position_code[:], parity[:])
+        parity_along_row = held.tile([D, BLOCK], BF16, name="parity_along_row", align_bytes=64)
+        nc.vector.memset(parity_along_row[:], 0.0)
+        nc.vector.memset(parity_along_row[:, 1::2], 1.0)
+        parity_by_partition = held.tile([D, BLOCK], BF16, name="parity_by_partition", align_bytes=64)
+        nc.vector.transpose(parity_by_partition[:], parity_along_row[:])
+        position_code = parity_by_partition[:, 0:1]
 
         pre = psum.tile([D, N], F32, name="pre")
-        nc.tensor.matmul(pre[:], x_weights[:], position_code[:].to_broadcast([D, N]), start=True, stop=False)
+        nc.tensor.matmul(pre[:], x_weights[:], position_code.to_broadcast([D, N]), start=True, stop=False)
         nc.tensor.matmul(pre[:], x_weights[:], x_tile[:], start=False, stop=False)
         nc.tensor.matmul(pre[:], node_weights[:], table_tile[:].indirect(offsets[:]), start=False, stop=True)
 

@@ -28,8 +28,9 @@ def tile_temporalattention_kernel(tc, table, x, w_node, w_x, b, offs, out):
         nc.scalar.dma_start(node_weights[:], w_node)
         table_tile = held.tile([D, S], BF16, name="table_tile")
         nc.scalar.dma_start(table_tile[:], table)
-        bias = held.tile([D, 1], F32, name="bias")
-        nc.scalar.dma_start(bias[:], b)
+        bias_along_row = held.tile([D, BLOCK], F32, name="bias_along_row", align_bytes=64)
+        nc.gpsimd.memset(bias_along_row[:], 0.0)
+        nc.scalar.dma_start(bias_along_row[0:D:BLOCK, :], b.rearrange("(q r) o -> q (r o)", r=BLOCK))
 
         scratch = held.tile([D, 1], F32, name="scratch")
         nc.vector.memset(scratch[:], 0.0)
@@ -42,11 +43,15 @@ def tile_temporalattention_kernel(tc, table, x, w_node, w_x, b, offs, out):
         nc.vector.transpose(parity_by_partition[:], parity_along_row[:])
         position_code = parity_by_partition[:, 0:1]
 
+        bias_by_partition = held.tile([D, BLOCK], F32, name="bias_by_partition", align_bytes=64)
+        nc.vector.transpose(bias_by_partition[:], bias_along_row[:])
+        bias = bias_by_partition[:, 0:1]
+
         pre = psum.tile([D, N], F32, name="pre")
         nc.tensor.matmul(pre[:], x_weights[:], position_code.to_broadcast([D, N]), start=True, stop=False)
         nc.tensor.matmul(pre[:], x_weights[:], x_tile[:], start=False, stop=False)
         nc.tensor.matmul(pre[:], node_weights[:], table_tile[:].indirect(offsets[:]), start=False, stop=True)
 
         result = held.tile([D, N], F32, name="result")
-        nc.scalar.activation(result[:], pre[:], mybir.ActivationFunctionType.Gelu, bias=bias[:])
+        nc.scalar.activation(result[:], pre[:], mybir.ActivationFunctionType.Gelu, bias=bias)
         nc.sync.dma_start(out, result[:])

import concourse.mybir as mybir

BF16 = mybir.dt.bfloat16
F32 = mybir.dt.float32
U16 = mybir.dt.uint16

D = 128
S = 256
N = 256
BLOCK = 32

FLOPS = 2 * D * D * N * 2 + 2 * (D // 2) * D


def tile_temporalattention_kernel(tc, table, x, w_node, w_x, b, offs, out):
    nc = tc.nc
    with (
        tc.tile_pool(name="held", bufs=1) as held,
        tc.psum_pool(name="psum", bufs=1) as psum,
    ):
        x_weights = held.tile([D, D], BF16, name="x_weights")
        nc.sync.dma_start(x_weights[:], w_x)
        x_tile = held.tile([D, N], BF16, name="x_tile")
        nc.sync.dma_start(x_tile[:], x)
        offsets = held.tile([D, N // 16], U16, name="offsets")
        nc.sync.dma_start(offsets[:], offs)
        node_weights = held.tile([D, D], BF16, name="node_weights")
        nc.scalar.dma_start(node_weights[:], w_node)
        table_tile = held.tile([D, S], BF16, name="table_tile")
        nc.scalar.dma_start(table_tile[:], table)
        bias_along_row = held.tile([D, BLOCK], F32, name="bias_along_row", align_bytes=64)
        nc.gpsimd.memset(bias_along_row[:], 0.0)
        nc.scalar.dma_start(bias_along_row[0:D:BLOCK, :], b.rearrange("(q r) o -> q (r o)", r=BLOCK))

        scratch = held.tile([D, 1], F32, name="scratch")
        nc.vector.memset(scratch[:], 0.0)
        nc.scalar.activation(scratch[:], scratch[:], mybir.ActivationFunctionType.Gelu)

        parity_along_row = held.tile([D, BLOCK], BF16, name="parity_along_row", align_bytes=64)
        nc.vector.memset(parity_along_row[:], 0.0)
        nc.vector.memset(parity_along_row[:, 1::2], 1.0)
        parity_by_partition = held.tile([D, BLOCK], BF16, name="parity_by_partition", align_bytes=64)
        nc.vector.transpose(parity_by_partition[:], parity_along_row[:])
        position_code = parity_by_partition[:, 0:1]

        bias_by_partition = held.tile([D, BLOCK], F32, name="bias_by_partition", align_bytes=64)
        nc.vector.transpose(bias_by_partition[:], bias_along_row[:])
        bias = bias_by_partition[:, 0:1]

        pre = psum.tile([D, N], F32, name="pre")
        nc.tensor.matmul(pre[:], x_weights[:], position_code.to_broadcast([D, N]), start=True, stop=False)
        nc.tensor.matmul(pre[:], x_weights[:], x_tile[:], start=False, stop=False)
        nc.tensor.matmul(pre[:], node_weights[:], table_tile[:].indirect(offsets[:]), start=False, stop=True)

        result = held.tile([D, N], F32, name="result")
        nc.scalar.activation(result[:], pre[:], mybir.ActivationFunctionType.Gelu, bias=bias)
        nc.sync.dma_start(out, result[:])
